import numpy as np
import ml_dtypes


def mxq(x, axis, fmt="e4m3"):
    dtype, down = {"e4m3": (ml_dtypes.float8_e4m3fn, 7), "e5m2": (ml_dtypes.float8_e5m2, 14)}[fmt]
    v = np.moveaxis(np.asarray(x, np.float32).astype(ml_dtypes.bfloat16).astype(np.float64), axis, -1)
    blocks = v.reshape(v.shape[:-1] + (-1, 32))
    amax = np.abs(blocks).max(-1, keepdims=True)
    byte = np.maximum(np.where(amax > 0, np.frexp(amax)[1] - 1 + 127, 0) - down, 1)
    scale = np.exp2(byte - 127.0)
    codes = (blocks / scale).astype(np.float32).astype(dtype).astype(np.float64)
    return np.moveaxis((codes * scale).reshape(v.shape), -1, axis)


WIDE = False


def mx_kscale(k):
    if not WIDE:
        return np.ones(k)
    levels = np.array([10, -10, 5, -5, 0])
    a = np.random.permutation(np.resize(levels, k // 512 * 4)).reshape(k // 512, 4)
    idx = np.arange(k)
    return np.exp2(a[idx // 512, idx % 128 // 32])


BF16 = ml_dtypes.bfloat16


def bf(x):
    return np.asarray(x, np.float32).astype(BF16)


def f64(x):
    return np.asarray(x).astype(np.float64)


E2M1 = np.array([0.0, 0.5, 1.0, 1.5, 2.0, 3.0, 4.0, 6.0, -0.0, -0.5, -1.0, -1.5, -2.0, -3.0, -4.0, -6.0])


def pack_weight(w, fmt):
    k, n = w.shape
    w = f64(bf(w)).reshape(k // 32, 32, n)
    amax = np.abs(w).max(1)
    if fmt == "e4m3":
        byte = np.frexp(amax)[1] - 1 + 127 - 7
    else:
        mant, ex = np.frexp(amax / 6.0)
        byte = np.where(mant > 0.5, ex, ex - 1) + 127
    byte = np.clip(np.where(amax > 0, byte, 1), 1, 254)
    scaled = (w * np.exp2(127.0 - byte)[:, None, :]).reshape(k, n).astype(np.float32)
    by_word = np.ascontiguousarray(scaled.reshape(k // 512, 128, 4, n).transpose(0, 1, 3, 2))
    if fmt == "e4m3":
        words = by_word.astype(ml_dtypes.float8_e4m3fn).view(np.uint8)
    else:
        c = by_word.astype(ml_dtypes.float4_e2m1fn).view(np.uint8) & 0xF
        words = c[..., 0::2] | (c[..., 1::2] << 4)
    return np.ascontiguousarray(words), np.ascontiguousarray(byte.astype(np.uint8).reshape(k // 512, 16, n))


def unpack_weight(words, scales, fmt):
    g, p, n, _ = words.shape
    if fmt == "e4m3":
        vals = np.ascontiguousarray(words).view(ml_dtypes.float8_e4m3fn).astype(np.float64)
    else:
        nib = np.empty((g, p, n, 4), np.uint8)
        nib[..., 0::2] = words & 0xF
        nib[..., 1::2] = words >> 4
        vals = E2M1[nib]
    vals = vals * np.repeat(np.exp2(scales.astype(np.float64) - 127.0), 8, axis=1)[..., None]
    return vals.transpose(0, 1, 3, 2).reshape(g * 512, n)

def pack4(w):
    words, scales = pack_weight(w, "e2m1")
    return words.reshape(words.shape[0], 128, -1), scales


def unpack4(words, scales):
    return unpack_weight(words.reshape(words.shape[0], 128, -1, 2), scales, "e2m1")


B, S, E, H = 2, 1024, 1024, 4
D = E // H
LN_EPS = 1e-6


def setup_inputs():
    s = mx_kscale(E)
    h_attn = bf(np.random.standard_normal((B, H, S, D)) * 0.4 * s.reshape(H, 1, D))
    x = bf(np.random.standard_normal((B, S, E)))
    out_w_words, out_w_scales = pack4(np.random.standard_normal((E, E)) * 2.0 / np.sqrt(E) / s[:, None])
    ln_gamma = bf(1.0 + 0.1 * np.random.standard_normal(E))
    ln_beta = bf(0.1 * np.random.standard_normal(E))
    return {"h_attn": h_attn,
            "x": x,
            "out_w_words": out_w_words,
            "out_w_scales": out_w_scales,
            "ln_gamma": ln_gamma,
            "ln_beta": ln_beta}


def reference(h_attn, x, out_w_words, out_w_scales, ln_gamma, ln_beta):
    merged = f64(h_attn).transpose(0, 2, 1, 3).reshape(B, S, E)
    out = mxq(merged, 2, "e4m3") @ unpack4(out_w_words, out_w_scales)
    y = out + f64(x)
    mean = y.mean(-1, keepdims=True)
    var = np.square(y - mean).mean(-1, keepdims=True)
    return (y - mean) / np.sqrt(var + LN_EPS) * f64(ln_gamma) + f64(ln_beta)

@@ -1,0 +1,187 @@
+from contextlib import ExitStack
+
+import concourse.masks as masks
+import concourse.mybir as mybir
+
+F32 = mybir.dt.float32
+BF16 = mybir.dt.bfloat16
+I32 = mybir.dt.int32
+U32 = mybir.dt.uint32
+U8 = mybir.dt.uint8
+FP8X4 = mybir.dt.float8_e4m3fn_x4
+FP4X4 = mybir.dt.float4_e2m1fn_x4
+ALU = mybir.AluOpType
+ACT = mybir.ActivationFunctionType
+
+B, H, S, D = 2, 4, 1024, 256
+E = H * D
+LN_EPS = 1e-6
+P = 128
+PACK = 4
+K_PASS = P * PACK
+PASSES = E // K_PASS
+WORDS_PASS = K_PASS // 2
+BANK = 512
+HALVES = E // BANK
+J = S // P
+TILES = B * J
+X_TILES = 2
+
+FLOPS = 2 * B * S * E * E
+
+
+def tile_selfattention_pa_kernel(tc, h_attn, x, out_w_words, out_w_scales, ln_gamma, ln_beta, out):
+    nc = tc.nc
+    h_view = h_attn.rearrange("b h (p j) d -> b j p h d", j=J)
+    x_view = x.rearrange("b (p j) e -> b p j e", j=J)
+    out_view = out.rearrange("b (p j) e -> b j p e", j=J)
+
+    with ExitStack() as ctx:
+        ctx.enter_context(tc.manual_schedule())
+        consts = ctx.enter_context(tc.tile_pool(name="consts", bufs=1))
+        loads = ctx.enter_context(tc.tile_pool(name="loads", bufs=1))
+        quant = ctx.enter_context(tc.tile_pool(name="quant", bufs=3))
+        work = ctx.enter_context(tc.tile_pool(name="work", bufs=4))
+        stats = ctx.enter_context(tc.tile_pool(name="stats", bufs=4))
+        affine_psum = ctx.enter_context(tc.psum_pool(name="affine_psum", bufs=1))
+        turn_psum = ctx.enter_context(tc.psum_pool(name="turn_psum", bufs=2))
+        acc_psum = ctx.enter_context(tc.psum_pool(name="acc_psum", bufs=2))
+
+        w_words = consts.tile([P, PASSES, 2 * E], U8, align_bytes=64)
+        w_scales = consts.tile([P, PASSES, E], U8, align_bytes=64)
+        nc.vector.memset(w_scales[:].bitcast(I32), 0)
+        scale_rows = out_w_scales.bitcast(I32)
+        for r in range(4):
+            nc.sync.dma_start(
+                out=w_scales[r:P:32, :, :].bitcast(I32),
+                in_=scale_rows[:, r:16:4, :].rearrange("g q n -> q g n"),
+            )
+
+        h_tiles = [loads.tile([P, E], BF16, name="h%d" % i) for i in range(TILES)]
+        x_tiles = [loads.tile([P, X_TILES, E], BF16, name="x%d" % c) for c in range(TILES // X_TILES)]
+
+        def load_h(i):
+            nc.sync.dma_start(
+                out=h_tiles[i][:].rearrange("p (h d) -> p h d", h=H), in_=h_view[i // J, i % J]
+            )
+
+        def load_x(c):
+            first = (c * X_TILES) % J
+            nc.sync.dma_start(out=x_tiles[c][:], in_=x_view[(c * X_TILES) // J, :, first : first + X_TILES, :])
+
+        load_h(0)
+        nc.sync.dma_start(
+            out=w_words[:].bitcast(I32), in_=out_w_words.bitcast(I32).rearrange("g p n -> p g n")
+        )
+        for c in range(TILES // X_TILES):
+            for i in range(c * X_TILES, (c + 1) * X_TILES):
+                if i > 0:
+                    load_h(i)
+            load_x(c)
+
+        affine_rows = consts.tile([P, 2, E], BF16)
+        nc.vector.memset(affine_rows[:], 0.0)
+        nc.scalar.dma_start(out=affine_rows[0:1, 0, :], in_=ln_gamma.unsqueeze(0))
+        nc.scalar.dma_start(out=affine_rows[0:1, 1, :], in_=ln_beta.unsqueeze(0))
+        ones = consts.tile([P, P], BF16)
+        nc.vector.memset(ones[:], 1.0)
+        gamma_all = affine_psum.tile([P, E], BF16)
+        beta_all = affine_psum.tile([P, E], BF16)
+        for row, spread in enumerate((gamma_all, beta_all)):
+            for n in range(HALVES):
+                cols = slice(n * BANK, (n + 1) * BANK)
+                nc.tensor.matmul(
+                    out=spread[:, cols], lhsT=ones[:], rhs=affine_rows[:, row, cols], start=True, stop=True
+                )
+
+        identity = consts.tile([P, P], F32)
+        masks.make_identity(nc, identity[:])
+        eps = consts.tile([P, 1], F32)
+        nc.vector.memset(eps[:], LN_EPS)
+        warm = consts.tile([P, 1], F32)
+        nc.scalar.activation(out=warm[:], in_=eps[:], func=ACT.Sqrt)
+
+        codes = {}
+        code_scales = {}
+        acc = {}
+        y = {}
+        neg_mean = {}
+        std = {}
+
+        def quantise(i):
+            h_words = h_tiles[i][:].bitcast(F32)
+            turned = turn_psum.tile([P, PASSES, 2, P], F32)
+            for g in range(PASSES):
+                for u in range(2):
+                    nc.tensor.transpose(
+                        turned[:, g, u, :], h_words[:, g * WORDS_PASS + u : (g + 1) * WORDS_PASS : 2], identity[:]
+                    )
+            grouped = quant.tile([P, PASSES, P, PACK], BF16, align_bytes=64)
+            nc.scalar.copy(out=grouped[:].bitcast(F32), in_=turned[:].rearrange("p g u t -> p g t u"))
+            codes[i] = quant.tile([P, PASSES * P], U32, name="codes", align_bytes=64)
+            code_scales[i] = quant.tile([P, PASSES * P], U8, name="code_scales", align_bytes=64)
+            nc.vector.quantize_mx(
+                out=codes[i][:].bitcast(FP8X4),
+                scales=code_scales[i][:],
+                in_=grouped[:].rearrange("p g t f -> p (g t f)"),
+            )
+
+        def project(i):
+            acc[i] = [acc_psum.tile([P, BANK], F32, name="acc%d" % n) for n in range(HALVES)]
+            for n in range(HALVES):
+                for g in range(PASSES):
+                    tokens = slice(g * P, (g + 1) * P)
+                    nc.tensor.matmul_mx(
+                        out=acc[i][n][:],
+                        lhsT=codes[i][:, tokens].bitcast(FP8X4),
+                        lhsT_scale=code_scales[i][:, tokens],
+                        rhs=w_words[:, g, n * 2 * BANK : (n + 1) * 2 * BANK].bitcast(FP4X4),
+                        rhs_scale=w_scales[:, g, n * BANK : (n + 1) * BANK],
+                        start=(g == 0),
+                        stop=(g == PASSES - 1),
+                    )
+
+        def residual_and_statistics(i):
+            y[i] = work.tile([P, E], F32, name="y")
+            y_sums = stats.tile([P, HALVES], F32)
+            for n in range(HALVES):
+                cols = slice(n * BANK, (n + 1) * BANK)
+                nc.vector.scalar_tensor_tensor(
+                    out=y[i][:, cols],
+                    in0=acc[i][n][:],
+                    scalar=1.0,
+                    in1=x_tiles[i // X_TILES][:, i % X_TILES, cols],
+                    op0=ALU.mult,
+                    op1=ALU.add,
+                    accum_out=y_sums[:, n : n + 1],
+                )
+            neg_mean[i] = stats.tile([P, 1], F32, name="neg_mean")
+            neg_parts = stats.tile([P, HALVES], F32)
+            nc.scalar.activation(
+                out=neg_parts[:], in_=y_sums[:], func=ACT.Copy, scale=-1.0 / E, accum_out=neg_mean[i][:]
+            )
+            squares = work.tile([P, E], BF16, bufs=2)
+            square_sum = stats.tile([P, 1], F32)
+            nc.scalar.activation(
+                out=squares[:], in_=y[i][:], func=ACT.Square, bias=neg_mean[i][:], accum_out=square_sum[:]
+            )
+            std[i] = stats.tile([P, 1], F32, name="std")
+            nc.scalar.activation(out=std[i][:], in_=square_sum[:], func=ACT.Sqrt, bias=eps[:], scale=1.0 / E)
+
+        def normalise_and_store(i):
+            inv_std = stats.tile([P, 1], F32)
+            nc.vector.reciprocal(out=inv_std[:], in_=std[i][:])
+            result = work.tile([P, E], F32)
+            nc.vector.scalar_tensor_tensor(
+                out=result[:], in0=y[i][:], scalar=neg_mean[i][:], in1=gamma_all[:], op0=ALU.add, op1=ALU.mult
+            )
+            nc.vector.scalar_tensor_tensor(
+                out=result[:], in0=result[:], scalar=inv_std[:], in1=beta_all[:], op0=ALU.mult, op1=ALU.add
+            )
+            nc.sync.dma_start(out=out_view[i // J, i % J], in_=result[:])
+
+        stages = (quantise, project, residual_and_statistics, normalise_and_store)
+        for step in range(TILES + len(stages) - 1):
+            for lag, stage in enumerate(stages):
+                if 0 <= step - lag < TILES:
+                    stage(step - lag)

@@ -23,9 +23,12 @@ PASSES = E // K_PASS
 WORDS_PASS = K_PASS // 2
 BANK = 512
 HALVES = E // BANK
+SPLIT = 512
+HIGH = slice(SPLIT, E)
 J = S // P
 TILES = B * J
 X_TILES = 2
+SHARED_TILES = TILES - 3
 
 FLOPS = 2 * B * S * E * E
 
@@ -37,93 +40,108 @@ def tile_selfattention_pa_kernel(tc, h_attn, x, out_w_words, out_w_scales, ln_ga
     out_view = out.rearrange("b (p j) e -> b j p e", j=J)
 
     with ExitStack() as ctx:
-        ctx.enter_context(tc.manual_schedule())
         consts = ctx.enter_context(tc.tile_pool(name="consts", bufs=1))
         loads = ctx.enter_context(tc.tile_pool(name="loads", bufs=1))
         quant = ctx.enter_context(tc.tile_pool(name="quant", bufs=3))
-        work = ctx.enter_context(tc.tile_pool(name="work", bufs=4))
-        stats = ctx.enter_context(tc.tile_pool(name="stats", bufs=4))
+        work = ctx.enter_context(tc.tile_pool(name="work", bufs=6))
+        stats = ctx.enter_context(tc.tile_pool(name="stats", bufs=8))
         affine_psum = ctx.enter_context(tc.psum_pool(name="affine_psum", bufs=1))
         turn_psum = ctx.enter_context(tc.psum_pool(name="turn_psum", bufs=2))
         acc_psum = ctx.enter_context(tc.psum_pool(name="acc_psum", bufs=2))
 
-        w_words = consts.tile([P, PASSES, 2 * E], U8, align_bytes=64)
         w_scales = consts.tile([P, PASSES, E], U8, align_bytes=64)
         nc.vector.memset(w_scales[:].bitcast(I32), 0)
+        identity = consts.tile([P, P], F32)
+        masks.make_identity(nc, identity[:])
+        affine_rows = consts.tile([P, 2, E], BF16)
+        nc.vector.memset(affine_rows[:], 0.0)
+        nc.gpsimd.dma_start(out=affine_rows[0:1, 0, :], in_=ln_gamma.unsqueeze(0))
+        nc.gpsimd.dma_start(out=affine_rows[0:1, 1, :], in_=ln_beta.unsqueeze(0))
+        ones = consts.tile([P, P], BF16)
+        nc.vector.memset(ones[:], 1.0)
+        eps = consts.tile([P, 1], F32)
+        nc.vector.memset(eps[:], LN_EPS)
+        warm = consts.tile([P, 1], F32)
+        nc.scalar.activation(out=warm[:], in_=eps[:], func=ACT.Abs_reciprocal_sqrt)
+
+        h_tiles = [loads.tile([P, E], BF16, name="h%d" % i) for i in range(TILES)]
+        x_tiles = [loads.tile([P, X_TILES, E], BF16, name="x%d" % c) for c in range(TILES // X_TILES)]
+        w_words = consts.tile([P, PASSES, 2 * E], U8, align_bytes=64)
+
+        def load_tokens(c):
+            for i in range(c * X_TILES, (c + 1) * X_TILES):
+                nc.sync.dma_start(
+                    out=h_tiles[i][:].rearrange("p (h d) -> p h d", h=H), in_=h_view[i // J, i % J]
+                )
+
+        def load_residual(c):
+            first = (c * X_TILES) % J
+            nc.sync.dma_start(out=x_tiles[c][:], in_=x_view[(c * X_TILES) // J, :, first : first + X_TILES, :])
+
+        load_tokens(0)
         scale_rows = out_w_scales.bitcast(I32)
         for r in range(4):
             nc.sync.dma_start(
                 out=w_scales[r:P:32, :, :].bitcast(I32),
                 in_=scale_rows[:, r:16:4, :].rearrange("g q n -> q g n"),
             )
-
-        h_tiles = [loads.tile([P, E], BF16, name="h%d" % i) for i in range(TILES)]
-        x_tiles = [loads.tile([P, X_TILES, E], BF16, name="x%d" % c) for c in range(TILES // X_TILES)]
-
-        def load_h(i):
-            nc.sync.dma_start(
-                out=h_tiles[i][:].rearrange("p (h d) -> p h d", h=H), in_=h_view[i // J, i % J]
-            )
-
-        def load_x(c):
-            first = (c * X_TILES) % J
-            nc.sync.dma_start(out=x_tiles[c][:], in_=x_view[(c * X_TILES) // J, :, first : first + X_TILES, :])
-
-        load_h(0)
         nc.sync.dma_start(
             out=w_words[:].bitcast(I32), in_=out_w_words.bitcast(I32).rearrange("g p n -> p g n")
         )
-        for c in range(TILES // X_TILES):
-            for i in range(c * X_TILES, (c + 1) * X_TILES):
-                if i > 0:
-                    load_h(i)
-            load_x(c)
+        load_residual(0)
+        for c in range(1, TILES // X_TILES):
+            load_tokens(c)
+            load_residual(c)
 
-        affine_rows = consts.tile([P, 2, E], BF16)
-        nc.vector.memset(affine_rows[:], 0.0)
-        nc.scalar.dma_start(out=affine_rows[0:1, 0, :], in_=ln_gamma.unsqueeze(0))
-        nc.scalar.dma_start(out=affine_rows[0:1, 1, :], in_=ln_beta.unsqueeze(0))
-        ones = consts.tile([P, P], BF16)
-        nc.vector.memset(ones[:], 1.0)
         gamma_all = affine_psum.tile([P, E], BF16)
         beta_all = affine_psum.tile([P, E], BF16)
-        for row, spread in enumerate((gamma_all, beta_all)):
-            for n in range(HALVES):
-                cols = slice(n * BANK, (n + 1) * BANK)
-                nc.tensor.matmul(
-                    out=spread[:, cols], lhsT=ones[:], rhs=affine_rows[:, row, cols], start=True, stop=True
-                )
+        affine_high = consts.tile([P, 2, E - SPLIT], F32)
 
-        identity = consts.tile([P, P], F32)
-        masks.make_identity(nc, identity[:])
-        eps = consts.tile([P, 1], F32)
-        nc.vector.memset(eps[:], LN_EPS)
-        warm = consts.tile([P, 1], F32)
-        nc.scalar.activation(out=warm[:], in_=eps[:], func=ACT.Sqrt)
+        def spread_affine():
+            for row, spread in enumerate((gamma_all, beta_all)):
+                for n in range(HALVES):
+                    cols = slice(n * BANK, (n + 1) * BANK)
+                    nc.tensor.matmul(
+                        out=spread[:, cols], lhsT=ones[:], rhs=affine_rows[:, row, cols], start=True, stop=True
+                    )
+                nc.scalar.copy(out=affine_high[:, row, :], in_=spread[:, HIGH])
 
+        def low(i):
+            return slice(0, SPLIT if i < SHARED_TILES else E)
+
+        turned = {}
+        grouped = {}
         codes = {}
         code_scales = {}
         acc = {}
         y = {}
+        y_sums = {}
         neg_mean = {}
-        std = {}
+        square_sum = {}
+        inv_std = {}
+        shift = {}
+        result = {}
 
-        def quantise(i):
+        def turn(i):
             h_words = h_tiles[i][:].bitcast(F32)
-            turned = turn_psum.tile([P, PASSES, 2, P], F32)
+            turned[i] = turn_psum.tile([P, PASSES, 2, P], F32, name="turned")
             for g in range(PASSES):
                 for u in range(2):
                     nc.tensor.transpose(
-                        turned[:, g, u, :], h_words[:, g * WORDS_PASS + u : (g + 1) * WORDS_PASS : 2], identity[:]
+                        turned[i][:, g, u, :], h_words[:, g * WORDS_PASS + u : (g + 1) * WORDS_PASS : 2], identity[:]
                     )
-            grouped = quant.tile([P, PASSES, P, PACK], BF16, align_bytes=64)
-            nc.scalar.copy(out=grouped[:].bitcast(F32), in_=turned[:].rearrange("p g u t -> p g t u"))
+
+        def regroup(i):
+            grouped[i] = quant.tile([P, PASSES, P, PACK], BF16, name="grouped", align_bytes=64)
+            nc.scalar.copy(out=grouped[i][:].bitcast(F32), in_=turned[i][:].rearrange("p g u t -> p g t u"))
+
+        def quantise(i):
             codes[i] = quant.tile([P, PASSES * P], U32, name="codes", align_bytes=64)
             code_scales[i] = quant.tile([P, PASSES * P], U8, name="code_scales", align_bytes=64)
             nc.vector.quantize_mx(
                 out=codes[i][:].bitcast(FP8X4),
                 scales=code_scales[i][:],
-                in_=grouped[:].rearrange("p g t f -> p (g t f)"),
+                in_=grouped[i][:].rearrange("p g t f -> p (g t f)"),
             )
 
         def project(i):
@@ -141,9 +159,9 @@ def tile_selfattention_pa_kernel(tc, h_attn, x, out_w_words, out_w_scales, ln_ga
                         stop=(g == PASSES - 1),
                     )
 
-        def residual_and_statistics(i):
+        def add_residual(i):
             y[i] = work.tile([P, E], F32, name="y")
-            y_sums = stats.tile([P, HALVES], F32)
+            y_sums[i] = stats.tile([P, HALVES], F32, name="y_sums")
             for n in range(HALVES):
                 cols = slice(n * BANK, (n + 1) * BANK)
                 nc.vector.scalar_tensor_tensor(
@@ -153,35 +171,79 @@ def tile_selfattention_pa_kernel(tc, h_attn, x, out_w_words, out_w_scales, ln_ga
                     in1=x_tiles[i // X_TILES][:, i % X_TILES, cols],
                     op0=ALU.mult,
                     op1=ALU.add,
-                    accum_out=y_sums[:, n : n + 1],
+                    accum_out=y_sums[i][:, n : n + 1],
                 )
+
+        def mean(i):
+            result[i] = work.tile([P, E], F32, name="result")
             neg_mean[i] = stats.tile([P, 1], F32, name="neg_mean")
             neg_parts = stats.tile([P, HALVES], F32)
             nc.scalar.activation(
-                out=neg_parts[:], in_=y_sums[:], func=ACT.Copy, scale=-1.0 / E, accum_out=neg_mean[i][:]
+                out=neg_parts[:], in_=y_sums[i][:], func=ACT.Copy, scale=-1.0 / E, accum_out=neg_mean[i][:]
             )
+
+        def sum_squares(i):
             squares = work.tile([P, E], BF16, bufs=2)
-            square_sum = stats.tile([P, 1], F32)
+            square_sum[i] = stats.tile([P, 1], F32, name="square_sum")
             nc.scalar.activation(
-                out=squares[:], in_=y[i][:], func=ACT.Square, bias=neg_mean[i][:], accum_out=square_sum[:]
+                out=squares[:], in_=y[i][:], func=ACT.Square, bias=neg_mean[i][:], accum_out=square_sum[i][:]
             )
-            std[i] = stats.tile([P, 1], F32, name="std")
-            nc.scalar.activation(out=std[i][:], in_=square_sum[:], func=ACT.Sqrt, bias=eps[:], scale=1.0 / E)
 
-        def normalise_and_store(i):
-            inv_std = stats.tile([P, 1], F32)
-            nc.vector.reciprocal(out=inv_std[:], in_=std[i][:])
-            result = work.tile([P, E], F32)
-            nc.vector.scalar_tensor_tensor(
-                out=result[:], in0=y[i][:], scalar=neg_mean[i][:], in1=gamma_all[:], op0=ALU.add, op1=ALU.mult
+        def deviation(i):
+            inv_std[i] = stats.tile([P, 1], F32, name="inv_std")
+            nc.scalar.activation(
+                out=inv_std[i][:], in_=square_sum[i][:], func=ACT.Abs_reciprocal_sqrt, bias=eps[:], scale=1.0 / E
             )
-            nc.vector.scalar_tensor_tensor(
-                out=result[:], in0=result[:], scalar=inv_std[:], in1=beta_all[:], op0=ALU.mult, op1=ALU.add
-            )
-            nc.sync.dma_start(out=out_view[i // J, i % J], in_=result[:])
 
-        stages = (quantise, project, residual_and_statistics, normalise_and_store)
-        for step in range(TILES + len(stages) - 1):
-            for lag, stage in enumerate(stages):
-                if 0 <= step - lag < TILES:
-                    stage(step - lag)
+        def normalise_high(i):
+            nc.scalar.activation(
+                out=result[i][:, HIGH], in_=y[i][:, HIGH], func=ACT.Identity, bias=shift[i][:], scale=inv_std[i][:]
+            )
+
+        def make_shift(i):
+            shift[i] = stats.tile([P, 1], F32, name="shift")
+            nc.scalar.activation(out=shift[i][:], in_=neg_mean[i][:], func=ACT.Copy, scale=inv_std[i][:])
+
+        def gamma_low(i):
+            nc.vector.scalar_tensor_tensor(
+                out=result[i][:, low(i)], in0=y[i][:, low(i)], scalar=neg_mean[i][:], in1=gamma_all[:, low(i)],
+                op0=ALU.add, op1=ALU.mult,
+            )
+
+        def beta_low(i):
+            nc.vector.scalar_tensor_tensor(
+                out=result[i][:, low(i)], in0=result[i][:, low(i)], scalar=inv_std[i][:], in1=beta_all[:, low(i)],
+                op0=ALU.mult, op1=ALU.add,
+            )
+
+        def gamma_high(i):
+            nc.gpsimd.tensor_tensor(out=result[i][:, HIGH], in0=result[i][:, HIGH], in1=affine_high[:, 0, :], op=ALU.mult)
+
+        def beta_high_and_store(i):
+            if i < SHARED_TILES:
+                nc.gpsimd.tensor_tensor(
+                    out=result[i][:, HIGH], in0=result[i][:, HIGH], in1=affine_high[:, 1, :], op=ALU.add
+                )
+            nc.sync.dma_start(out=out_view[i // J, i % J], in_=result[i][:])
+
+        def when_in_range(stage, i, tiles=TILES):
+            if 0 <= i < tiles:
+                stage(i)
+
+        for step in range(TILES + 7):
+            when_in_range(turn, step)
+            when_in_range(mean, step - 4)
+            when_in_range(make_shift, step - 5, SHARED_TILES)
+            when_in_range(add_residual, step - 3)
+            when_in_range(regroup, step)
+            if step == 1:
+                spread_affine()
+            when_in_range(sum_squares, step - 4)
+            when_in_range(normalise_high, step - 5, SHARED_TILES)
+            when_in_range(deviation, step - 4)
+            when_in_range(gamma_low, step - 5)
+            when_in_range(beta_low, step - 6)
+            when_in_range(quantise, step - 1)
+            when_in_range(project, step - 1)
+            when_in_range(gamma_high, step - 6, SHARED_TILES)
+            when_in_range(beta_high_and_store, step - 7)

@@ -24,6 +24,7 @@ WORDS_PASS = K_PASS // 2
 BANK = 512
 HALVES = E // BANK
 SPLIT = 512
+LOW = slice(0, SPLIT)
 HIGH = slice(SPLIT, E)
 J = S // P
 TILES = B * J
@@ -40,6 +41,7 @@ def tile_selfattention_pa_kernel(tc, h_attn, x, out_w_words, out_w_scales, ln_ga
     out_view = out.rearrange("b (p j) e -> b j p e", j=J)
 
     with ExitStack() as ctx:
+        ctx.enter_context(tc.manual_schedule())
         consts = ctx.enter_context(tc.tile_pool(name="consts", bufs=1))
         loads = ctx.enter_context(tc.tile_pool(name="loads", bufs=1))
         quant = ctx.enter_context(tc.tile_pool(name="quant", bufs=3))
@@ -106,8 +108,11 @@ def tile_selfattention_pa_kernel(tc, h_attn, x, out_w_words, out_w_scales, ln_ga
                     )
                 nc.scalar.copy(out=affine_high[:, row, :], in_=spread[:, HIGH])
 
-        def low(i):
-            return slice(0, SPLIT if i < SHARED_TILES else E)
+        def vector_parts(i):
+            return (LOW,) if i < SHARED_TILES else (LOW, HIGH)
+
+        def store(i, cols):
+            nc.sync.dma_start(out=out_view[i // J, i % J][:, cols], in_=result[i][:, cols])
 
         turned = {}
         grouped = {}
@@ -204,46 +209,46 @@ def tile_selfattention_pa_kernel(tc, h_attn, x, out_w_words, out_w_scales, ln_ga
             shift[i] = stats.tile([P, 1], F32, name="shift")
             nc.scalar.activation(out=shift[i][:], in_=neg_mean[i][:], func=ACT.Copy, scale=inv_std[i][:])
 
-        def gamma_low(i):
-            nc.vector.scalar_tensor_tensor(
-                out=result[i][:, low(i)], in0=y[i][:, low(i)], scalar=neg_mean[i][:], in1=gamma_all[:, low(i)],
-                op0=ALU.add, op1=ALU.mult,
-            )
+        def gamma_vector(i):
+            for cols in vector_parts(i):
+                nc.vector.scalar_tensor_tensor(
+                    out=result[i][:, cols], in0=y[i][:, cols], scalar=neg_mean[i][:], in1=gamma_all[:, cols],
+                    op0=ALU.add, op1=ALU.mult,
+                )
 
-        def beta_low(i):
-            nc.vector.scalar_tensor_tensor(
-                out=result[i][:, low(i)], in0=result[i][:, low(i)], scalar=inv_std[i][:], in1=beta_all[:, low(i)],
-                op0=ALU.mult, op1=ALU.add,
-            )
+        def beta_vector_and_store(i):
+            for cols in vector_parts(i):
+                nc.vector.scalar_tensor_tensor(
+                    out=result[i][:, cols], in0=result[i][:, cols], scalar=inv_std[i][:], in1=beta_all[:, cols],
+                    op0=ALU.mult, op1=ALU.add,
+                )
+                store(i, cols)
 
         def gamma_high(i):
             nc.gpsimd.tensor_tensor(out=result[i][:, HIGH], in0=result[i][:, HIGH], in1=affine_high[:, 0, :], op=ALU.mult)
 
         def beta_high_and_store(i):
-            if i < SHARED_TILES:
-                nc.gpsimd.tensor_tensor(
-                    out=result[i][:, HIGH], in0=result[i][:, HIGH], in1=affine_high[:, 1, :], op=ALU.add
-                )
-            nc.sync.dma_start(out=out_view[i // J, i % J], in_=result[i][:])
+            nc.gpsimd.tensor_tensor(out=result[i][:, HIGH], in0=result[i][:, HIGH], in1=affine_high[:, 1, :], op=ALU.add)
+            store(i, HIGH)
 
         def when_in_range(stage, i, tiles=TILES):
             if 0 <= i < tiles:
                 stage(i)
 
-        for step in range(TILES + 7):
+        for step in range(TILES + 6):
             when_in_range(turn, step)
             when_in_range(mean, step - 4)
             when_in_range(make_shift, step - 5, SHARED_TILES)
             when_in_range(add_residual, step - 3)
             when_in_range(regroup, step)
-            if step == 1:
+            if step == 3:
                 spread_affine()
             when_in_range(sum_squares, step - 4)
             when_in_range(normalise_high, step - 5, SHARED_TILES)
             when_in_range(deviation, step - 4)
-            when_in_range(gamma_low, step - 5)
-            when_in_range(beta_low, step - 6)
+            when_in_range(gamma_vector, step - 5)
+            when_in_range(beta_vector_and_store, step - 6)
             when_in_range(quantise, step - 1)
             when_in_range(project, step - 1)
             when_in_range(gamma_high, step - 6, SHARED_TILES)
-            when_in_range(beta_high_and_store, step - 7)
+            when_in_range(beta_high_and_store, step - 7, SHARED_TILES)

@@ -23,13 +23,13 @@ PASSES = E // K_PASS
 WORDS_PASS = K_PASS // 2
 BANK = 512
 HALVES = E // BANK
-SPLIT = 512
-LOW = slice(0, SPLIT)
-HIGH = slice(SPLIT, E)
+LOW = slice(0, BANK)
+HIGH = slice(BANK, E)
+WHOLE = slice(0, E)
 J = S // P
 TILES = B * J
 X_TILES = 2
-SHARED_TILES = TILES - 3
+GPSIMD_TILES = tuple(range(0, TILES - 2, 2))
 
 FLOPS = 2 * B * S * E * E
 
@@ -57,8 +57,6 @@ def tile_selfattention_pa_kernel(tc, h_attn, x, out_w_words, out_w_scales, ln_ga
         masks.make_identity(nc, identity[:])
         affine_rows = consts.tile([P, 2, E], BF16)
         nc.vector.memset(affine_rows[:], 0.0)
-        nc.gpsimd.dma_start(out=affine_rows[0:1, 0, :], in_=ln_gamma.unsqueeze(0))
-        nc.gpsimd.dma_start(out=affine_rows[0:1, 1, :], in_=ln_beta.unsqueeze(0))
         ones = consts.tile([P, P], BF16)
         nc.vector.memset(ones[:], 1.0)
         eps = consts.tile([P, 1], F32)
@@ -91,13 +89,15 @@ def tile_selfattention_pa_kernel(tc, h_attn, x, out_w_words, out_w_scales, ln_ga
             out=w_words[:].bitcast(I32), in_=out_w_words.bitcast(I32).rearrange("g p n -> p g n")
         )
         load_residual(0)
+        nc.sync.dma_start(out=affine_rows[0:1, 0, :], in_=ln_gamma.unsqueeze(0))
+        nc.sync.dma_start(out=affine_rows[0:1, 1, :], in_=ln_beta.unsqueeze(0))
         for c in range(1, TILES // X_TILES):
             load_tokens(c)
             load_residual(c)
 
         gamma_all = affine_psum.tile([P, E], BF16)
         beta_all = affine_psum.tile([P, E], BF16)
-        affine_high = consts.tile([P, 2, E - SPLIT], F32)
+        affine_sbuf = consts.tile([P, 2, E], F32)
 
         def spread_affine():
             for row, spread in enumerate((gamma_all, beta_all)):
@@ -106,10 +106,10 @@ def tile_selfattention_pa_kernel(tc, h_attn, x, out_w_words, out_w_scales, ln_ga
                     nc.tensor.matmul(
                         out=spread[:, cols], lhsT=ones[:], rhs=affine_rows[:, row, cols], start=True, stop=True
                     )
-                nc.scalar.copy(out=affine_high[:, row, :], in_=spread[:, HIGH])
+                nc.scalar.copy(out=affine_sbuf[:, row, :], in_=spread[:])
 
         def vector_parts(i):
-            return (LOW,) if i < SHARED_TILES else (LOW, HIGH)
+            return (WHOLE,) if i < TILES - 1 else (LOW, HIGH)
 
         def store(i, cols):
             nc.sync.dma_start(out=out_view[i // J, i % J][:, cols], in_=result[i][:, cols])
@@ -202,7 +202,7 @@ def tile_selfattention_pa_kernel(tc, h_attn, x, out_w_words, out_w_scales, ln_ga
 
         def normalise_high(i):
             nc.scalar.activation(
-                out=result[i][:, HIGH], in_=y[i][:, HIGH], func=ACT.Identity, bias=shift[i][:], scale=inv_std[i][:]
+                out=result[i][:], in_=y[i][:], func=ACT.Identity, bias=shift[i][:], scale=inv_std[i][:]
             )
 
         def make_shift(i):
@@ -225,30 +225,38 @@ def tile_selfattention_pa_kernel(tc, h_attn, x, out_w_words, out_w_scales, ln_ga
                 store(i, cols)
 
         def gamma_high(i):
-            nc.gpsimd.tensor_tensor(out=result[i][:, HIGH], in0=result[i][:, HIGH], in1=affine_high[:, 0, :], op=ALU.mult)
+            nc.gpsimd.tensor_tensor(out=result[i][:], in0=result[i][:], in1=affine_sbuf[:, 0, :], op=ALU.mult)
 
         def beta_high_and_store(i):
-            nc.gpsimd.tensor_tensor(out=result[i][:, HIGH], in0=result[i][:, HIGH], in1=affine_high[:, 1, :], op=ALU.add)
-            store(i, HIGH)
+            nc.gpsimd.tensor_tensor(out=result[i][:], in0=result[i][:], in1=affine_sbuf[:, 1, :], op=ALU.add)
+            store(i, WHOLE)
 
-        def when_in_range(stage, i, tiles=TILES):
-            if 0 <= i < tiles:
+        def when_in_range(stage, i):
+            if 0 <= i < TILES:
+                stage(i)
+
+        def for_gpsimd(stage, i):
+            if i in GPSIMD_TILES:
+                stage(i)
+
+        def for_vector(stage, i):
+            if 0 <= i < TILES and i not in GPSIMD_TILES:
                 stage(i)
 
         for step in range(TILES + 6):
             when_in_range(turn, step)
-            when_in_range(mean, step - 4)
-            when_in_range(make_shift, step - 5, SHARED_TILES)
             when_in_range(add_residual, step - 3)
+            when_in_range(mean, step - 3)
+            for_gpsimd(make_shift, step - 4)
             when_in_range(regroup, step)
-            if step == 3:
+            if step == 2:
                 spread_affine()
-            when_in_range(sum_squares, step - 4)
-            when_in_range(normalise_high, step - 5, SHARED_TILES)
-            when_in_range(deviation, step - 4)
-            when_in_range(gamma_vector, step - 5)
-            when_in_range(beta_vector_and_store, step - 6)
+            when_in_range(sum_squares, step - 3)
+            for_gpsimd(normalise_high, step - 4)
+            when_in_range(deviation, step - 3)
+            for_vector(gamma_vector, step - 4)
+            for_vector(beta_vector_and_store, step - 5)
             when_in_range(quantise, step - 1)
             when_in_range(project, step - 1)
-            when_in_range(gamma_high, step - 6, SHARED_TILES)
-            when_in_range(beta_high_and_store, step - 7, SHARED_TILES)
+            for_gpsimd(gamma_high, step - 4)
+            for_gpsimd(beta_high_and_store, step - 5)

@@ -180,7 +180,7 @@ def tile_selfattention_pa_kernel(tc, h_attn, x, out_w_words, out_w_scales, ln_ga
                 )
 
         def mean(i):
-            result[i] = work.tile([P, E], F32, name="result")
+            result[i] = work.tile([P, E], F32, name="result", bufs=TILES)
             neg_mean[i] = stats.tile([P, 1], F32, name="neg_mean")
             neg_parts = stats.tile([P, HALVES], F32)
             nc.scalar.activation(

@@ -108,8 +108,8 @@ def tile_selfattention_pa_kernel(tc, h_attn, x, out_w_words, out_w_scales, ln_ga
                     )
                 nc.scalar.copy(out=affine_sbuf[:, row, :], in_=spread[:])
 
-        def vector_parts(i):
-            return (WHOLE,) if i < TILES - 1 else (LOW, HIGH)
+        def parts(i):
+            return (LOW, HIGH) if i == GPSIMD_TILES[-1] or i >= TILES - 2 else (WHOLE,)
 
         def store(i, cols):
             nc.sync.dma_start(out=out_view[i // J, i % J][:, cols], in_=result[i][:, cols])
@@ -210,14 +210,14 @@ def tile_selfattention_pa_kernel(tc, h_attn, x, out_w_words, out_w_scales, ln_ga
             nc.scalar.activation(out=shift[i][:], in_=neg_mean[i][:], func=ACT.Copy, scale=inv_std[i][:])
 
         def gamma_vector(i):
-            for cols in vector_parts(i):
+            for cols in parts(i):
                 nc.vector.scalar_tensor_tensor(
                     out=result[i][:, cols], in0=y[i][:, cols], scalar=neg_mean[i][:], in1=gamma_all[:, cols],
                     op0=ALU.add, op1=ALU.mult,
                 )
 
         def beta_vector_and_store(i):
-            for cols in vector_parts(i):
+            for cols in parts(i):
                 nc.vector.scalar_tensor_tensor(
                     out=result[i][:, cols], in0=result[i][:, cols], scalar=inv_std[i][:], in1=beta_all[:, cols],
                     op0=ALU.mult, op1=ALU.add,
@@ -228,8 +228,17 @@ def tile_selfattention_pa_kernel(tc, h_attn, x, out_w_words, out_w_scales, ln_ga
             nc.gpsimd.tensor_tensor(out=result[i][:], in0=result[i][:], in1=affine_sbuf[:, 0, :], op=ALU.mult)
 
         def beta_high_and_store(i):
-            nc.gpsimd.tensor_tensor(out=result[i][:], in0=result[i][:], in1=affine_sbuf[:, 1, :], op=ALU.add)
-            store(i, WHOLE)
+            for cols in parts(i):
+                nc.gpsimd.tensor_tensor(
+                    out=result[i][:, cols], in0=result[i][:, cols], in1=affine_sbuf[:, 1, cols], op=ALU.add
+                )
+
+        def store_first(i):
+            if len(parts(i)) > 1:
+                store(i, parts(i)[0])
+
+        def store_last(i):
+            store(i, parts(i)[-1])
 
         def when_in_range(stage, i):
             if 0 <= i < TILES:
@@ -260,3 +269,5 @@ def tile_selfattention_pa_kernel(tc, h_attn, x, out_w_words, out_w_scales, ln_ga
             when_in_range(project, step - 1)
             for_gpsimd(gamma_high, step - 4)
             for_gpsimd(beta_high_and_store, step - 5)
+            for_gpsimd(store_first, step - 6)
+            for_gpsimd(store_last, step - 7)

@@ -112,7 +112,8 @@ def tile_selfattention_pa_kernel(tc, h_attn, x, out_w_words, out_w_scales, ln_ga
             return (LOW, HIGH) if i == GPSIMD_TILES[-1] or i >= TILES - 2 else (WHOLE,)
 
         def store(i, cols):
-            nc.sync.dma_start(out=out_view[i // J, i % J][:, cols], in_=result[i][:, cols])
+            queue = nc.scalar if i == GPSIMD_TILES[-1] else nc.sync
+            queue.dma_start(out=out_view[i // J, i % J][:, cols], in_=result[i][:, cols])
 
         turned = {}
         grouped = {}
@@ -263,8 +264,8 @@ def tile_selfattention_pa_kernel(tc, h_attn, x, out_w_words, out_w_scales, ln_ga
             when_in_range(sum_squares, step - 3)
             for_gpsimd(normalise_high, step - 4)
             when_in_range(deviation, step - 3)
-            for_vector(gamma_vector, step - 4)
             for_vector(beta_vector_and_store, step - 5)
+            for_vector(gamma_vector, step - 4)
             when_in_range(quantise, step - 1)
             when_in_range(project, step - 1)
             for_gpsimd(gamma_high, step - 4)

from contextlib import ExitStack

import concourse.masks as masks
import concourse.mybir as mybir

F32 = mybir.dt.float32
BF16 = mybir.dt.bfloat16
I32 = mybir.dt.int32
U32 = mybir.dt.uint32
U8 = mybir.dt.uint8
FP8X4 = mybir.dt.float8_e4m3fn_x4
FP4X4 = mybir.dt.float4_e2m1fn_x4
ALU = mybir.AluOpType
ACT = mybir.ActivationFunctionType

B, H, S, D = 2, 4, 1024, 256
E = H * D
LN_EPS = 1e-6
P = 128
PACK = 4
K_PASS = P * PACK
PASSES = E // K_PASS
WORDS_PASS = K_PASS // 2
BANK = 512
HALVES = E // BANK
LOW = slice(0, BANK)
HIGH = slice(BANK, E)
WHOLE = slice(0, E)
J = S // P
TILES = B * J
X_TILES = 2
GPSIMD_TILES = tuple(range(0, TILES - 2, 2))

FLOPS = 2 * B * S * E * E


def tile_selfattention_pa_kernel(tc, h_attn, x, out_w_words, out_w_scales, ln_gamma, ln_beta, out):
    nc = tc.nc
    h_view = h_attn.rearrange("b h (p j) d -> b j p h d", j=J)
    x_view = x.rearrange("b (p j) e -> b p j e", j=J)
    out_view = out.rearrange("b (p j) e -> b j p e", j=J)

    with ExitStack() as ctx:
        ctx.enter_context(tc.manual_schedule())
        consts = ctx.enter_context(tc.tile_pool(name="consts", bufs=1))
        loads = ctx.enter_context(tc.tile_pool(name="loads", bufs=1))
        quant = ctx.enter_context(tc.tile_pool(name="quant", bufs=3))
        work = ctx.enter_context(tc.tile_pool(name="work", bufs=6))
        stats = ctx.enter_context(tc.tile_pool(name="stats", bufs=8))
        affine_psum = ctx.enter_context(tc.psum_pool(name="affine_psum", bufs=1))
        turn_psum = ctx.enter_context(tc.psum_pool(name="turn_psum", bufs=2))
        acc_psum = ctx.enter_context(tc.psum_pool(name="acc_psum", bufs=2))

        w_scales = consts.tile([P, PASSES, E], U8, align_bytes=64)
        nc.vector.memset(w_scales[:].bitcast(I32), 0)
        identity = consts.tile([P, P], F32)
        masks.make_identity(nc, identity[:])
        affine_rows = consts.tile([P, 2, E], BF16)
        nc.vector.memset(affine_rows[:], 0.0)
        ones = consts.tile([P, P], BF16)
        nc.vector.memset(ones[:], 1.0)
        eps = consts.tile([P, 1], F32)
        nc.vector.memset(eps[:], LN_EPS)
        warm = consts.tile([P, 1], F32)
        nc.scalar.activation(out=warm[:], in_=eps[:], func=ACT.Abs_reciprocal_sqrt)

        h_tiles = [loads.tile([P, E], BF16, name="h%d" % i) for i in range(TILES)]
        x_tiles = [loads.tile([P, X_TILES, E], BF16, name="x%d" % c) for c in range(TILES // X_TILES)]
        w_words = consts.tile([P, PASSES, 2 * E], U8, align_bytes=64)

        def load_tokens(c):
            for i in range(c * X_TILES, (c + 1) * X_TILES):
                nc.sync.dma_start(
                    out=h_tiles[i][:].rearrange("p (h d) -> p h d", h=H), in_=h_view[i // J, i % J]
                )

        def load_residual(c):
            first = (c * X_TILES) % J
            nc.sync.dma_start(out=x_tiles[c][:], in_=x_view[(c * X_TILES) // J, :, first : first + X_TILES, :])

        load_tokens(0)
        scale_rows = out_w_scales.bitcast(I32)
        for r in range(4):
            nc.sync.dma_start(
                out=w_scales[r:P:32, :, :].bitcast(I32),
                in_=scale_rows[:, r:16:4, :].rearrange("g q n -> q g n"),
            )
        nc.sync.dma_start(
            out=w_words[:].bitcast(I32), in_=out_w_words.bitcast(I32).rearrange("g p n -> p g n")
        )
        load_residual(0)
        nc.sync.dma_start(out=affine_rows[0:1, 0, :], in_=ln_gamma.unsqueeze(0))
        nc.sync.dma_start(out=affine_rows[0:1, 1, :], in_=ln_beta.unsqueeze(0))
        for c in range(1, TILES // X_TILES):
            load_tokens(c)
            load_residual(c)

        gamma_all = affine_psum.tile([P, E], BF16)
        beta_all = affine_psum.tile([P, E], BF16)
        affine_sbuf = consts.tile([P, 2, E], F32)

        def spread_affine():
            for row, spread in enumerate((gamma_all, beta_all)):
                for n in range(HALVES):
                    cols = slice(n * BANK, (n + 1) * BANK)
                    nc.tensor.matmul(
                        out=spread[:, cols], lhsT=ones[:], rhs=affine_rows[:, row, cols], start=True, stop=True
                    )
                nc.scalar.copy(out=affine_sbuf[:, row, :], in_=spread[:])

        def parts(i):
            return (LOW, HIGH) if i == GPSIMD_TILES[-1] or i >= TILES - 2 else (WHOLE,)

        def store(i, cols):
            queue = nc.scalar if i == GPSIMD_TILES[-1] else nc.sync
            queue.dma_start(out=out_view[i // J, i % J][:, cols], in_=result[i][:, cols])

        turned = {}
        grouped = {}
        codes = {}
        code_scales = {}
        acc = {}
        y = {}
        y_sums = {}
        neg_mean = {}
        square_sum = {}
        inv_std = {}
        shift = {}
        result = {}

        def turn(i):
            h_words = h_tiles[i][:].bitcast(F32)
            turned[i] = turn_psum.tile([P, PASSES, 2, P], F32, name="turned")
            for g in range(PASSES):
                for u in range(2):
                    nc.tensor.transpose(
                        turned[i][:, g, u, :], h_words[:, g * WORDS_PASS + u : (g + 1) * WORDS_PASS : 2], identity[:]
                    )

        def regroup(i):
            grouped[i] = quant.tile([P, PASSES, P, PACK], BF16, name="grouped", align_bytes=64)
            nc.scalar.copy(out=grouped[i][:].bitcast(F32), in_=turned[i][:].rearrange("p g u t -> p g t u"))

        def quantise(i):
            codes[i] = quant.tile([P, PASSES * P], U32, name="codes", align_bytes=64)
            code_scales[i] = quant.tile([P, PASSES * P], U8, name="code_scales", align_bytes=64)
            nc.vector.quantize_mx(
                out=codes[i][:].bitcast(FP8X4),
                scales=code_scales[i][:],
                in_=grouped[i][:].rearrange("p g t f -> p (g t f)"),
            )

        def project(i):
            acc[i] = [acc_psum.tile([P, BANK], F32, name="acc%d" % n) for n in range(HALVES)]
            for n in range(HALVES):
                for g in range(PASSES):
                    tokens = slice(g * P, (g + 1) * P)
                    nc.tensor.matmul_mx(
                        out=acc[i][n][:],
                        lhsT=codes[i][:, tokens].bitcast(FP8X4),
                        lhsT_scale=code_scales[i][:, tokens],
                        rhs=w_words[:, g, n * 2 * BANK : (n + 1) * 2 * BANK].bitcast(FP4X4),
                        rhs_scale=w_scales[:, g, n * BANK : (n + 1) * BANK],
                        start=(g == 0),
                        stop=(g == PASSES - 1),
                    )

        def add_residual(i):
            y[i] = work.tile([P, E], F32, name="y")
            y_sums[i] = stats.tile([P, HALVES], F32, name="y_sums")
            for n in range(HALVES):
                cols = slice(n * BANK, (n + 1) * BANK)
                nc.vector.scalar_tensor_tensor(
                    out=y[i][:, cols],
                    in0=acc[i][n][:],
                    scalar=1.0,
                    in1=x_tiles[i // X_TILES][:, i % X_TILES, cols],
                    op0=ALU.mult,
                    op1=ALU.add,
                    accum_out=y_sums[i][:, n : n + 1],
                )

        def mean(i):
            result[i] = work.tile([P, E], F32, name="result", bufs=TILES)
            neg_mean[i] = stats.tile([P, 1], F32, name="neg_mean")
            neg_parts = stats.tile([P, HALVES], F32)
            nc.scalar.activation(
                out=neg_parts[:], in_=y_sums[i][:], func=ACT.Copy, scale=-1.0 / E, accum_out=neg_mean[i][:]
            )

        def sum_squares(i):
            squares = work.tile([P, E], BF16, bufs=2)
            square_sum[i] = stats.tile([P, 1], F32, name="square_sum")
            nc.scalar.activation(
                out=squares[:], in_=y[i][:], func=ACT.Square, bias=neg_mean[i][:], accum_out=square_sum[i][:]
            )

        def deviation(i):
            inv_std[i] = stats.tile([P, 1], F32, name="inv_std")
            nc.scalar.activation(
                out=inv_std[i][:], in_=square_sum[i][:], func=ACT.Abs_reciprocal_sqrt, bias=eps[:], scale=1.0 / E
            )

        def normalise_high(i):
            nc.scalar.activation(
                out=result[i][:], in_=y[i][:], func=ACT.Identity, bias=shift[i][:], scale=inv_std[i][:]
            )

        def make_shift(i):
            shift[i] = stats.tile([P, 1], F32, name="shift")
            nc.scalar.activation(out=shift[i][:], in_=neg_mean[i][:], func=ACT.Copy, scale=inv_std[i][:])

        def gamma_vector(i):
            for cols in parts(i):
                nc.vector.scalar_tensor_tensor(
                    out=result[i][:, cols], in0=y[i][:, cols], scalar=neg_mean[i][:], in1=gamma_all[:, cols],
                    op0=ALU.add, op1=ALU.mult,
                )

        def beta_vector_and_store(i):
            for cols in parts(i):
                nc.vector.scalar_tensor_tensor(
                    out=result[i][:, cols], in0=result[i][:, cols], scalar=inv_std[i][:], in1=beta_all[:, cols],
                    op0=ALU.mult, op1=ALU.add,
                )
                store(i, cols)

        def gamma_high(i):
            nc.gpsimd.tensor_tensor(out=result[i][:], in0=result[i][:], in1=affine_sbuf[:, 0, :], op=ALU.mult)

        def beta_high_and_store(i):
            for cols in parts(i):
                nc.gpsimd.tensor_tensor(
                    out=result[i][:, cols], in0=result[i][:, cols], in1=affine_sbuf[:, 1, cols], op=ALU.add
                )

        def store_first(i):
            if len(parts(i)) > 1:
                store(i, parts(i)[0])

        def store_last(i):
            store(i, parts(i)[-1])

        def when_in_range(stage, i):
            if 0 <= i < TILES:
                stage(i)

        def for_gpsimd(stage, i):
            if i in GPSIMD_TILES:
                stage(i)

        def for_vector(stage, i):
            if 0 <= i < TILES and i not in GPSIMD_TILES:
                stage(i)

        for step in range(TILES + 6):
            when_in_range(turn, step)
            when_in_range(add_residual, step - 3)
            when_in_range(mean, step - 3)
            for_gpsimd(make_shift, step - 4)
            when_in_range(regroup, step)
            if step == 2:
                spread_affine()
            when_in_range(sum_squares, step - 3)
            for_gpsimd(normalise_high, step - 4)
            when_in_range(deviation, step - 3)
            for_vector(beta_vector_and_store, step - 5)
            for_vector(gamma_vector, step - 4)
            when_in_range(quantise, step - 1)
            when_in_range(project, step - 1)
            for_gpsimd(gamma_high, step - 4)
            for_gpsimd(beta_high_and_store, step - 5)
            for_gpsimd(store_first, step - 6)
            for_gpsimd(store_last, step - 7)
